import numpy as np
import ml_dtypes


def mxq(x, axis, fmt="e4m3"):
    dtype, down = {"e4m3": (ml_dtypes.float8_e4m3fn, 7), "e5m2": (ml_dtypes.float8_e5m2, 14)}[fmt]
    v = np.moveaxis(np.asarray(x, np.float32).astype(ml_dtypes.bfloat16).astype(np.float64), axis, -1)
    blocks = v.reshape(v.shape[:-1] + (-1, 32))
    amax = np.abs(blocks).max(-1, keepdims=True)
    byte = np.maximum(np.where(amax > 0, np.frexp(amax)[1] - 1 + 127, 0) - down, 1)
    scale = np.exp2(byte - 127.0)
    codes = (blocks / scale).astype(np.float32).astype(dtype).astype(np.float64)
    return np.moveaxis((codes * scale).reshape(v.shape), -1, axis)


WIDE = False


def mx_kscale(k):
    if not WIDE:
        return np.ones(k)
    levels = np.array([10, -10, 5, -5, 0])
    a = np.random.permutation(np.resize(levels, k // 512 * 4)).reshape(k // 512, 4)
    idx = np.arange(k)
    return np.exp2(a[idx // 512, idx % 128 // 32])


BF16 = ml_dtypes.bfloat16


def bf(x):
    return np.asarray(x, np.float32).astype(BF16)


def f64(x):
    return np.asarray(x).astype(np.float64)


B, C, H, W, K = 32, 256, 16, 32, 128
N = H * W
XS = 1.6 / C ** 0.25
CS = 0.4 / C ** 0.25


def setup_inputs():
    s = mx_kscale(N)
    z = 1.3 * np.random.standard_normal((B, N, K)) + np.random.standard_normal((1, 1, K))
    a = np.exp(z - z.max(axis=-1, keepdims=True))
    a = a / a.sum(axis=-1, keepdims=True)
    feat = XS * (np.random.standard_normal((B, N, C)) + 0.4 * np.random.standard_normal((1, 1, C)))
    return {'assign': bf(a * s[None, :, None]),
            'xp': bf(feat / s[None, :, None]),
            'codebook': bf(np.random.standard_normal((K, C)) * CS / s.mean())}


def reference(assign, xp, codebook):
    assign, xp, codebook = f64(assign), f64(xp), f64(codebook)
    a_sum = np.sum(assign, axis=1)
    e = (mxq(assign, 1, 'e4m3').transpose(0, 2, 1) @ mxq(xp, 1, 'e4m3')) - a_sum[:, :, None] * codebook[None]
    return e

@@ -1,0 +1,176 @@
+from contextlib import ExitStack
+
+import concourse.mybir as mybir
+
+FP8X4 = mybir.dt.float8_e4m3fn_x4
+BF16 = mybir.dt.bfloat16
+F32 = mybir.dt.float32
+U32 = mybir.dt.uint32
+U8 = mybir.dt.uint8
+MULT = mybir.AluOpType.mult
+ADD = mybir.AluOpType.add
+
+B, N, K, C = 32, 512, 128, 256
+P = 128
+PACK = 4
+FLOPS = 2 * B * N * K * C
+
+LOAD_SIZES = [1, 1, 2, 4, 4, 4, 4, 4, 4, 4]
+UNIT_SIZES = [1, 1, 2, 4, 4, 4, 4, 4, 4, 2, 1, 1]
+GMAX = 4
+
+
+def tile_lvc_pb_t_kernel(tc, assign, xp, codebook, out):
+    nc = tc.nc
+    a_view = assign.rearrange("b (p j) k -> p b (j k)", j=PACK)
+    x_view = xp.rearrange("b (p j) c -> p b (j c)", j=PACK)
+    o_view = out.rearrange("b k c -> k b c")
+
+    units = []
+    b0 = 0
+    for g in UNIT_SIZES:
+        units.append((b0, g))
+        b0 += g
+    n_units = len(units)
+
+    with ExitStack() as ctx:
+        keep = ctx.enter_context(tc.tile_pool(name="keep", bufs=1))
+        gx_pool = ctx.enter_context(tc.tile_pool(name="gx_pool", bufs=3))
+        ga_pool = ctx.enter_context(tc.tile_pool(name="ga_pool", bufs=3))
+        qx_pool = ctx.enter_context(tc.tile_pool(name="qx_pool", bufs=3))
+        qa_pool = ctx.enter_context(tc.tile_pool(name="qa_pool", bufs=4))
+        psum = ctx.enter_context(tc.psum_pool(name="psum", bufs=8))
+        ctx.enter_context(tc.manual_schedule())
+
+        neg_ones = keep.tile([P, 1], BF16, name="neg_ones")
+        nc.vector.memset(neg_ones[:], -1.0)
+        cb = keep.tile([P, C], BF16, name="cb")
+        nc.scalar.dma_start(out=cb[:], in_=codebook)
+
+        raw_a = {}
+        raw_x = {}
+        b0 = 0
+        for i, g in enumerate(LOAD_SIZES):
+            ta = keep.tile([P, g, PACK * K], BF16, name="raw_a%d" % i)
+            nc.sync.dma_start(out=ta[:], in_=a_view[:, b0:b0 + g, :])
+            tx = keep.tile([P, g, PACK * C], BF16, name="raw_x%d" % i)
+            nc.sync.dma_start(out=tx[:], in_=x_view[:, b0:b0 + g, :])
+            for r in range(g):
+                raw_a[b0 + r] = (ta, r)
+                raw_x[b0 + r] = (tx, r)
+            b0 += g
+
+        ga = {}
+        gx = {}
+        qa = {}
+        qx = {}
+        ps = {}
+
+        def regroup_a(u):
+            b0, g = units[u]
+            t = ga_pool.tile([P, GMAX, K * PACK], BF16, name="ga", align_bytes=64)
+            ga[u] = t
+            src, r = raw_a[b0]
+            nc.vector.tensor_copy(
+                out=t[:, 0:g, :].rearrange("p g (c i t) -> p g c t i", i=4, t=PACK),
+                in_=src[:, r:r + g, :].rearrange("p g (t c i) -> p g c t i", i=4, t=PACK),
+            )
+
+        def quant_a(u):
+            b0, g = units[u]
+            codes = qa_pool.tile([P, GMAX * K], U32, name="ca", align_bytes=64)
+            scales = qa_pool.tile([P, GMAX * K], U8, name="sa", align_bytes=64)
+            qa[u] = (codes, scales)
+            nc.vector.quantize_mx(
+                out=codes[:, 0:g * K].bitcast(FP8X4),
+                scales=scales[:, 0:g * K],
+                in_=ga[u][:, 0:g, :].rearrange("p g e -> p (g e)"),
+            )
+
+        def regroup_x(u):
+            b0, g = units[u]
+            t = gx_pool.tile([P, GMAX, C * PACK], BF16, name="gx", align_bytes=64)
+            gx[u] = t
+            for r in range(g):
+                src, rr = raw_x[b0 + r]
+                nc.scalar.copy(
+                    out=t[:, r, :].rearrange("p (c i t) -> p c t i", i=4, t=PACK),
+                    in_=src[:, rr, :].rearrange("p (t c i) -> p c t i", i=4, t=PACK),
+                )
+
+        def quant_x(u):
+            b0, g = units[u]
+            codes = qx_pool.tile([P, GMAX * C], U32, name="cx", align_bytes=64)
+            scales = qx_pool.tile([P, GMAX * C], U8, name="sx", align_bytes=64)
+            qx[u] = (codes, scales)
+            nc.vector.quantize_mx(
+                out=codes[:, 0:g * C].bitcast(FP8X4),
+                scales=scales[:, 0:g * C],
+                in_=gx[u][:, 0:g, :].rearrange("p g e -> p (g e)"),
+            )
+
+        def sums(u):
+            b0, g = units[u]
+            for r in range(g):
+                acc = psum.tile([P, 512], F32, name="acc")
+                ps[b0 + r] = acc
+                src, rr = raw_a[b0 + r]
+                for j in range(PACK):
+                    nc.tensor.matmul(
+                        out=acc[:, C:C + 1],
+                        lhsT=src[:, rr, j * K:(j + 1) * K],
+                        rhs=neg_ones[:, 0:1],
+                        start=(j == 0),
+                        stop=(j == PACK - 1),
+                    )
+
+        def products(u):
+            b0, g = units[u]
+            ca, sa = qa[u]
+            cx, sx = qx[u]
+            for r in range(g):
+                nc.tensor.matmul_mx(
+                    out=ps[b0 + r][:, 0:C],
+                    lhsT=ca[:, r * K:(r + 1) * K].bitcast(FP8X4),
+                    lhsT_scale=sa[:, r * K:(r + 1) * K],
+                    rhs=cx[:, r * C:(r + 1) * C].bitcast(FP8X4),
+                    rhs_scale=sx[:, r * C:(r + 1) * C],
+                    start=True,
+                    stop=True,
+                )
+
+        def finish(u):
+            b0, g = units[u]
+            res = keep.tile([P, g, C], F32, name="res%d" % u)
+            for r in range(g):
+                acc = ps[b0 + r]
+                nc.vector.scalar_tensor_tensor(
+                    out=res[:, r, :],
+                    in0=cb[:],
+                    scalar=acc[:, C:C + 1],
+                    in1=acc[:, 0:C],
+                    op0=MULT,
+                    op1=ADD,
+                )
+            nc.sync.dma_start(out=o_view[:, b0:b0 + g, :], in_=res[:])
+
+        regroup_a(0)
+        regroup_a(1)
+        quant_a(0)
+        regroup_a(2)
+        quant_a(1)
+        regroup_x(0)
+        regroup_x(1)
+        sums(0)
+        for u in range(n_units):
+            quant_x(u)
+            if u + 2 < n_units:
+                regroup_x(u + 2)
+            if u + 3 < n_units:
+                regroup_a(u + 3)
+            if u + 1 < n_units:
+                sums(u + 1)
+            products(u)
+            finish(u)
+            if u + 2 < n_units:
+                quant_a(u + 2)

@@ -15,9 +15,9 @@ P = 128
 PACK = 4
 FLOPS = 2 * B * N * K * C
 
-LOAD_SIZES = [1, 1, 2, 4, 4, 4, 4, 4, 4, 4]
-UNIT_SIZES = [1, 1, 2, 4, 4, 4, 4, 4, 4, 2, 1, 1]
-GMAX = 4
+UNIT_SIZES = [1, 1, 1, 1] + [2] * 12 + [1, 1, 1, 1]
+LOAD_SIZES = UNIT_SIZES
+GMAX = 2
 
 
 def tile_lvc_pb_t_kernel(tc, assign, xp, codebook, out):
@@ -51,10 +51,10 @@ def tile_lvc_pb_t_kernel(tc, assign, xp, codebook, out):
         raw_x = {}
         b0 = 0
         for i, g in enumerate(LOAD_SIZES):
-            ta = keep.tile([P, g, PACK * K], BF16, name="raw_a%d" % i)
-            nc.sync.dma_start(out=ta[:], in_=a_view[:, b0:b0 + g, :])
             tx = keep.tile([P, g, PACK * C], BF16, name="raw_x%d" % i)
             nc.sync.dma_start(out=tx[:], in_=x_view[:, b0:b0 + g, :])
+            ta = keep.tile([P, g, PACK * K], BF16, name="raw_a%d" % i)
+            nc.sync.dma_start(out=ta[:], in_=a_view[:, b0:b0 + g, :])
             for r in range(g):
                 raw_a[b0 + r] = (ta, r)
                 raw_x[b0 + r] = (tx, r)
@@ -154,23 +154,17 @@ def tile_lvc_pb_t_kernel(tc, assign, xp, codebook, out):
                 )
             nc.sync.dma_start(out=o_view[:, b0:b0 + g, :], in_=res[:])
 
-        regroup_a(0)
-        regroup_a(1)
-        quant_a(0)
-        regroup_a(2)
-        quant_a(1)
-        regroup_x(0)
-        regroup_x(1)
-        sums(0)
-        for u in range(n_units):
-            quant_x(u)
-            if u + 2 < n_units:
-                regroup_x(u + 2)
-            if u + 3 < n_units:
-                regroup_a(u + 3)
-            if u + 1 < n_units:
-                sums(u + 1)
-            products(u)
-            finish(u)
-            if u + 2 < n_units:
-                quant_a(u + 2)
+        for u in range(n_units + 2):
+            if u < n_units:
+                regroup_x(u)
+            if 1 <= u <= n_units:
+                quant_x(u - 1)
+            if u < n_units:
+                regroup_a(u)
+            if u >= 2:
+                finish(u - 2)
+            if 1 <= u <= n_units:
+                sums(u - 1)
+                products(u - 1)
+            if u < n_units:
+                quant_a(u)

@@ -16,7 +16,8 @@ PACK = 4
 FLOPS = 2 * B * N * K * C
 
 UNIT_SIZES = [1, 1, 1, 1] + [2] * 12 + [1, 1, 1, 1]
-LOAD_SIZES = UNIT_SIZES
+LOAD_SIZES = [1, 1, 1, 1] + [2] * 6 + [4] * 4
+STORE_SIZES = [4] * 7 + [2, 1, 1]
 GMAX = 2
 
 
@@ -58,6 +59,14 @@ def tile_lvc_pb_t_kernel(tc, assign, xp, codebook, out):
             for r in range(g):
                 raw_a[b0 + r] = (ta, r)
                 raw_x[b0 + r] = (tx, r)
+            b0 += g
+
+        res_of = {}
+        b0 = 0
+        for i, g in enumerate(STORE_SIZES):
+            tr = keep.tile([P, g, C], F32, name="res%d" % i)
+            for r in range(g):
+                res_of[b0 + r] = (tr, r, b0, g)
             b0 += g
 
         ga = {}
@@ -141,18 +150,19 @@ def tile_lvc_pb_t_kernel(tc, assign, xp, codebook, out):
 
         def finish(u):
             b0, g = units[u]
-            res = keep.tile([P, g, C], F32, name="res%d" % u)
             for r in range(g):
                 acc = ps[b0 + r]
+                res, rr, s0, sg = res_of[b0 + r]
                 nc.vector.scalar_tensor_tensor(
-                    out=res[:, r, :],
+                    out=res[:, rr, :],
                     in0=cb[:],
                     scalar=acc[:, C:C + 1],
                     in1=acc[:, 0:C],
                     op0=MULT,
                     op1=ADD,
                 )
-            nc.sync.dma_start(out=o_view[:, b0:b0 + g, :], in_=res[:])
+                if rr == sg - 1:
+                    nc.sync.dma_start(out=o_view[:, s0:s0 + sg, :], in_=res[:])
 
         for u in range(n_units + 2):
             if u < n_units:

@@ -19,6 +19,7 @@ UNIT_SIZES = [1, 1, 1, 1] + [2] * 12 + [1, 1, 1, 1]
 LOAD_SIZES = [1, 1, 1, 1] + [2] * 6 + [4] * 4
 STORE_SIZES = [4] * 7 + [2, 1, 1]
 GMAX = 2
+VECTOR_X = (9, 19)
 
 
 def tile_lvc_pb_t_kernel(tc, assign, xp, codebook, out):
@@ -101,9 +102,22 @@ def tile_lvc_pb_t_kernel(tc, assign, xp, codebook, out):
             t = gx_pool.tile([P, GMAX, C * PACK], BF16, name="gx", align_bytes=64)
             gx[u] = t
             for r in range(g):
+                if b0 + r in VECTOR_X:
+                    continue
                 src, rr = raw_x[b0 + r]
                 nc.scalar.copy(
                     out=t[:, r, :].rearrange("p (c i t) -> p c t i", i=4, t=PACK),
+                    in_=src[:, rr, :].rearrange("p (t c i) -> p c t i", i=4, t=PACK),
+                )
+
+        def regroup_x_vector(u):
+            b0, g = units[u]
+            for r in range(g):
+                if b0 + r not in VECTOR_X:
+                    continue
+                src, rr = raw_x[b0 + r]
+                nc.vector.tensor_copy(
+                    out=gx[u][:, r, :].rearrange("p (c i t) -> p c t i", i=4, t=PACK),
                     in_=src[:, rr, :].rearrange("p (t c i) -> p c t i", i=4, t=PACK),
                 )
 
@@ -170,6 +184,7 @@ def tile_lvc_pb_t_kernel(tc, assign, xp, codebook, out):
             if 1 <= u <= n_units:
                 quant_x(u - 1)
             if u < n_units:
+                regroup_x_vector(u)
                 regroup_a(u)
             if u >= 2:
                 finish(u - 2)

@@ -19,6 +19,7 @@ UNIT_SIZES = [1, 1, 1, 1] + [2] * 12 + [1, 1, 1, 1]
 LOAD_SIZES = [1, 1, 1, 1] + [2] * 6 + [4] * 4
 STORE_SIZES = [4] * 7 + [2, 1, 1]
 GMAX = 2
+RUN = 8
 VECTOR_X = (9, 19)
 
 
@@ -82,8 +83,8 @@ def tile_lvc_pb_t_kernel(tc, assign, xp, codebook, out):
             ga[u] = t
             src, r = raw_a[b0]
             nc.vector.tensor_copy(
-                out=t[:, 0:g, :].rearrange("p g (c i t) -> p g c t i", i=4, t=PACK),
-                in_=src[:, r:r + g, :].rearrange("p g (t c i) -> p g c t i", i=4, t=PACK),
+                out=t[:, 0:g, :].rearrange("p g (c i t) -> p g c t i", i=RUN, t=PACK),
+                in_=src[:, r:r + g, :].rearrange("p g (t c i) -> p g c t i", i=RUN, t=PACK),
             )
 
         def quant_a(u):
@@ -106,8 +107,8 @@ def tile_lvc_pb_t_kernel(tc, assign, xp, codebook, out):
                     continue
                 src, rr = raw_x[b0 + r]
                 nc.scalar.copy(
-                    out=t[:, r, :].rearrange("p (c i t) -> p c t i", i=4, t=PACK),
-                    in_=src[:, rr, :].rearrange("p (t c i) -> p c t i", i=4, t=PACK),
+                    out=t[:, r, :].rearrange("p (c i t) -> p c t i", i=RUN, t=PACK),
+                    in_=src[:, rr, :].rearrange("p (t c i) -> p c t i", i=RUN, t=PACK),
                 )
 
         def regroup_x_vector(u):
@@ -117,8 +118,8 @@ def tile_lvc_pb_t_kernel(tc, assign, xp, codebook, out):
                     continue
                 src, rr = raw_x[b0 + r]
                 nc.vector.tensor_copy(
-                    out=gx[u][:, r, :].rearrange("p (c i t) -> p c t i", i=4, t=PACK),
-                    in_=src[:, rr, :].rearrange("p (t c i) -> p c t i", i=4, t=PACK),
+                    out=gx[u][:, r, :].rearrange("p (c i t) -> p c t i", i=RUN, t=PACK),
+                    in_=src[:, rr, :].rearrange("p (t c i) -> p c t i", i=RUN, t=PACK),
                 )
 
         def quant_x(u):

@@ -184,13 +184,11 @@ def tile_lvc_pb_t_kernel(tc, assign, xp, codebook, out):
                 regroup_x(u)
             if 1 <= u <= n_units:
                 quant_x(u - 1)
+                quant_a(u - 1)
+                sums(u - 1)
+                products(u - 1)
+            if u >= 2:
+                finish(u - 2)
             if u < n_units:
                 regroup_x_vector(u)
                 regroup_a(u)
-            if u >= 2:
-                finish(u - 2)
-            if 1 <= u <= n_units:
-                sums(u - 1)
-                products(u - 1)
-            if u < n_units:
-                quant_a(u)

from contextlib import ExitStack

import concourse.mybir as mybir

FP8X4 = mybir.dt.float8_e4m3fn_x4
BF16 = mybir.dt.bfloat16
F32 = mybir.dt.float32
U32 = mybir.dt.uint32
U8 = mybir.dt.uint8
MULT = mybir.AluOpType.mult
ADD = mybir.AluOpType.add

B, N, K, C = 32, 512, 128, 256
P = 128
PACK = 4
FLOPS = 2 * B * N * K * C

UNIT_SIZES = [1, 1, 1, 1] + [2] * 12 + [1, 1, 1, 1]
LOAD_SIZES = [1, 1, 1, 1] + [2] * 6 + [4] * 4
STORE_SIZES = [4] * 7 + [2, 1, 1]
GMAX = 2
RUN = 8
VECTOR_X = (9, 19)


def tile_lvc_pb_t_kernel(tc, assign, xp, codebook, out):
    nc = tc.nc
    a_view = assign.rearrange("b (p j) k -> p b (j k)", j=PACK)
    x_view = xp.rearrange("b (p j) c -> p b (j c)", j=PACK)
    o_view = out.rearrange("b k c -> k b c")

    units = []
    b0 = 0
    for g in UNIT_SIZES:
        units.append((b0, g))
        b0 += g
    n_units = len(units)

    with ExitStack() as ctx:
        keep = ctx.enter_context(tc.tile_pool(name="keep", bufs=1))
        gx_pool = ctx.enter_context(tc.tile_pool(name="gx_pool", bufs=3))
        ga_pool = ctx.enter_context(tc.tile_pool(name="ga_pool", bufs=3))
        qx_pool = ctx.enter_context(tc.tile_pool(name="qx_pool", bufs=3))
        qa_pool = ctx.enter_context(tc.tile_pool(name="qa_pool", bufs=4))
        psum = ctx.enter_context(tc.psum_pool(name="psum", bufs=8))
        ctx.enter_context(tc.manual_schedule())

        neg_ones = keep.tile([P, 1], BF16, name="neg_ones")
        nc.vector.memset(neg_ones[:], -1.0)
        cb = keep.tile([P, C], BF16, name="cb")
        nc.scalar.dma_start(out=cb[:], in_=codebook)

        raw_a = {}
        raw_x = {}
        b0 = 0
        for i, g in enumerate(LOAD_SIZES):
            tx = keep.tile([P, g, PACK * C], BF16, name="raw_x%d" % i)
            nc.sync.dma_start(out=tx[:], in_=x_view[:, b0:b0 + g, :])
            ta = keep.tile([P, g, PACK * K], BF16, name="raw_a%d" % i)
            nc.sync.dma_start(out=ta[:], in_=a_view[:, b0:b0 + g, :])
            for r in range(g):
                raw_a[b0 + r] = (ta, r)
                raw_x[b0 + r] = (tx, r)
            b0 += g

        res_of = {}
        b0 = 0
        for i, g in enumerate(STORE_SIZES):
            tr = keep.tile([P, g, C], F32, name="res%d" % i)
            for r in range(g):
                res_of[b0 + r] = (tr, r, b0, g)
            b0 += g

        ga = {}
        gx = {}
        qa = {}
        qx = {}
        ps = {}

        def regroup_a(u):
            b0, g = units[u]
            t = ga_pool.tile([P, GMAX, K * PACK], BF16, name="ga", align_bytes=64)
            ga[u] = t
            src, r = raw_a[b0]
            nc.vector.tensor_copy(
                out=t[:, 0:g, :].rearrange("p g (c i t) -> p g c t i", i=RUN, t=PACK),
                in_=src[:, r:r + g, :].rearrange("p g (t c i) -> p g c t i", i=RUN, t=PACK),
            )

        def quant_a(u):
            b0, g = units[u]
            codes = qa_pool.tile([P, GMAX * K], U32, name="ca", align_bytes=64)
            scales = qa_pool.tile([P, GMAX * K], U8, name="sa", align_bytes=64)
            qa[u] = (codes, scales)
            nc.vector.quantize_mx(
                out=codes[:, 0:g * K].bitcast(FP8X4),
                scales=scales[:, 0:g * K],
                in_=ga[u][:, 0:g, :].rearrange("p g e -> p (g e)"),
            )

        def regroup_x(u):
            b0, g = units[u]
            t = gx_pool.tile([P, GMAX, C * PACK], BF16, name="gx", align_bytes=64)
            gx[u] = t
            for r in range(g):
                if b0 + r in VECTOR_X:
                    continue
                src, rr = raw_x[b0 + r]
                nc.scalar.copy(
                    out=t[:, r, :].rearrange("p (c i t) -> p c t i", i=RUN, t=PACK),
                    in_=src[:, rr, :].rearrange("p (t c i) -> p c t i", i=RUN, t=PACK),
                )

        def regroup_x_vector(u):
            b0, g = units[u]
            for r in range(g):
                if b0 + r not in VECTOR_X:
                    continue
                src, rr = raw_x[b0 + r]
                nc.vector.tensor_copy(
                    out=gx[u][:, r, :].rearrange("p (c i t) -> p c t i", i=RUN, t=PACK),
                    in_=src[:, rr, :].rearrange("p (t c i) -> p c t i", i=RUN, t=PACK),
                )

        def quant_x(u):
            b0, g = units[u]
            codes = qx_pool.tile([P, GMAX * C], U32, name="cx", align_bytes=64)
            scales = qx_pool.tile([P, GMAX * C], U8, name="sx", align_bytes=64)
            qx[u] = (codes, scales)
            nc.vector.quantize_mx(
                out=codes[:, 0:g * C].bitcast(FP8X4),
                scales=scales[:, 0:g * C],
                in_=gx[u][:, 0:g, :].rearrange("p g e -> p (g e)"),
            )

        def sums(u):
            b0, g = units[u]
            for r in range(g):
                acc = psum.tile([P, 512], F32, name="acc")
                ps[b0 + r] = acc
                src, rr = raw_a[b0 + r]
                for j in range(PACK):
                    nc.tensor.matmul(
                        out=acc[:, C:C + 1],
                        lhsT=src[:, rr, j * K:(j + 1) * K],
                        rhs=neg_ones[:, 0:1],
                        start=(j == 0),
                        stop=(j == PACK - 1),
                    )

        def products(u):
            b0, g = units[u]
            ca, sa = qa[u]
            cx, sx = qx[u]
            for r in range(g):
                nc.tensor.matmul_mx(
                    out=ps[b0 + r][:, 0:C],
                    lhsT=ca[:, r * K:(r + 1) * K].bitcast(FP8X4),
                    lhsT_scale=sa[:, r * K:(r + 1) * K],
                    rhs=cx[:, r * C:(r + 1) * C].bitcast(FP8X4),
                    rhs_scale=sx[:, r * C:(r + 1) * C],
                    start=True,
                    stop=True,
                )

        def finish(u):
            b0, g = units[u]
            for r in range(g):
                acc = ps[b0 + r]
                res, rr, s0, sg = res_of[b0 + r]
                nc.vector.scalar_tensor_tensor(
                    out=res[:, rr, :],
                    in0=cb[:],
                    scalar=acc[:, C:C + 1],
                    in1=acc[:, 0:C],
                    op0=MULT,
                    op1=ADD,
                )
                if rr == sg - 1:
                    nc.sync.dma_start(out=o_view[:, s0:s0 + sg, :], in_=res[:])

        for u in range(n_units + 2):
            if u < n_units:
                regroup_x(u)
            if 1 <= u <= n_units:
                quant_x(u - 1)
                quant_a(u - 1)
                sums(u - 1)
                products(u - 1)
            if u >= 2:
                finish(u - 2)
            if u < n_units:
                regroup_x_vector(u)
                regroup_a(u)
